import numpy as np
import ml_dtypes


def mxq(x, axis, fmt="e4m3"):
    dtype, down = {"e4m3": (ml_dtypes.float8_e4m3fn, 7), "e5m2": (ml_dtypes.float8_e5m2, 14)}[fmt]
    v = np.moveaxis(np.asarray(x, np.float32).astype(ml_dtypes.bfloat16).astype(np.float64), axis, -1)
    blocks = v.reshape(v.shape[:-1] + (-1, 32))
    amax = np.abs(blocks).max(-1, keepdims=True)
    byte = np.maximum(np.where(amax > 0, np.frexp(amax)[1] - 1 + 127, 0) - down, 1)
    scale = np.exp2(byte - 127.0)
    codes = (blocks / scale).astype(np.float32).astype(dtype).astype(np.float64)
    return np.moveaxis((codes * scale).reshape(v.shape), -1, axis)


WIDE = False


def mx_kscale(k):
    if not WIDE:
        return np.ones(k)
    levels = np.array([10, -10, 5, -5, 0])
    a = np.random.permutation(np.resize(levels, k // 512 * 4)).reshape(k // 512, 4)
    idx = np.arange(k)
    return np.exp2(a[idx // 512, idx % 128 // 32])


BF16 = ml_dtypes.bfloat16


def bf(x):
    return np.asarray(x, np.float32).astype(BF16)


def f64(x):
    return np.asarray(x).astype(np.float64)


E2M1 = np.array([0.0, 0.5, 1.0, 1.5, 2.0, 3.0, 4.0, 6.0, -0.0, -0.5, -1.0, -1.5, -2.0, -3.0, -4.0, -6.0])


def pack_weight(w, fmt):
    k, n = w.shape
    w = f64(bf(w)).reshape(k // 32, 32, n)
    amax = np.abs(w).max(1)
    if fmt == "e4m3":
        byte = np.frexp(amax)[1] - 1 + 127 - 7
    else:
        mant, ex = np.frexp(amax / 6.0)
        byte = np.where(mant > 0.5, ex, ex - 1) + 127
    byte = np.clip(np.where(amax > 0, byte, 1), 1, 254)
    scaled = (w * np.exp2(127.0 - byte)[:, None, :]).reshape(k, n).astype(np.float32)
    by_word = np.ascontiguousarray(scaled.reshape(k // 512, 128, 4, n).transpose(0, 1, 3, 2))
    if fmt == "e4m3":
        words = by_word.astype(ml_dtypes.float8_e4m3fn).view(np.uint8)
    else:
        c = by_word.astype(ml_dtypes.float4_e2m1fn).view(np.uint8) & 0xF
        words = c[..., 0::2] | (c[..., 1::2] << 4)
    return np.ascontiguousarray(words), np.ascontiguousarray(byte.astype(np.uint8).reshape(k // 512, 16, n))


def unpack_weight(words, scales, fmt):
    g, p, n, _ = words.shape
    if fmt == "e4m3":
        vals = np.ascontiguousarray(words).view(ml_dtypes.float8_e4m3fn).astype(np.float64)
    else:
        nib = np.empty((g, p, n, 4), np.uint8)
        nib[..., 0::2] = words & 0xF
        nib[..., 1::2] = words >> 4
        vals = E2M1[nib]
    vals = vals * np.repeat(np.exp2(scales.astype(np.float64) - 127.0), 8, axis=1)[..., None]
    return vals.transpose(0, 1, 3, 2).reshape(g * 512, n)


B, O, I, LQ, LS, D = 256, 2, 16, 32, 32, 16
FS = LS * D
KV = I * LS
EPS = 1e-5
SHIFT = 14.0


def setup_inputs():
    s = mx_kscale(FS)
    enc = np.random.standard_normal((B, I, FS)) * s
    scores = bf(-SHIFT + 1.5 * np.random.standard_normal((B, O, I, LQ, LS)))
    wv = np.random.standard_normal((O, FS, FS)) * 1.5 / np.sqrt(FS) / s
    cat = np.ascontiguousarray(np.swapaxes(wv, 1, 2)).reshape(-1, FS)
    words, scales = pack_weight(cat, "e4m3")
    return {
        "scores": scores,
        "final_encoder_out": bf(enc.reshape(B, I * LS, D)),
        "WV_w_words": words,
        "WV_w_scales": scales,
        "WV_b": bf(np.random.standard_normal((O, FS)) * 0.2),
    }


def reference(scores, final_encoder_out, WV_w_words, WV_w_scales, WV_b):
    encq = mxq(f64(final_encoder_out).reshape(B * I, FS), 1, "e4m3")
    wkn = unpack_weight(WV_w_words, WV_w_scales, "e4m3").reshape(O, FS, FS).transpose(1, 0, 2).reshape(FS, O * FS)
    v = (encq @ wkn) + f64(WV_b).reshape(O * FS)
    v = np.swapaxes(v.reshape(B, I, O, LS, D), 1, 2).reshape(B, O, KV, D)
    e = np.exp(f64(scores))
    attn = e / (e.sum(-1, keepdims=True) + EPS)
    attn = np.swapaxes(attn, 2, 3).reshape(B, O, LQ, KV)
    z = mxq(attn, 3, "e4m3") @ mxq(v, 2, "e4m3")
    coeff = 1.0 / np.sqrt(D)
    return (coeff * z).reshape(B, O * LQ, D)

@@ -1,0 +1,327 @@
+import math
+from contextlib import ExitStack
+
+import concourse.mybir as mybir
+from concourse.masks import make_identity
+
+F32 = mybir.dt.float32
+BF16 = mybir.dt.bfloat16
+I32 = mybir.dt.int32
+U32 = mybir.dt.uint32
+U8 = mybir.dt.uint8
+FP8X4 = mybir.dt.float8_e4m3fn_x4
+ACT = mybir.ActivationFunctionType
+ALU = mybir.AluOpType
+AXIS = mybir.AxisListType
+
+P = 128
+PACK = 4
+B, O, I, LQ, LS, D = 256, 2, 16, 32, 32, 16
+FS = LS * D
+EPS = 1e-5
+A = I // PACK
+
+B_TILE = P // (O * PACK)
+N_TILES = B // B_TILE
+Q_CHUNK = 8
+N_CHUNKS = LQ // Q_CHUNK
+B_PASS = P // LQ
+PASSES = B_TILE // B_PASS
+STORE_TILES = 4
+
+B_GROUP = P // PACK
+N_GROUPS = B // B_GROUP
+ROW_TILES = B_GROUP * I // P
+B_ROWS = P // I
+N_UNITS = N_GROUPS * O
+B_MOVING = P // D
+D_CHUNK = 8
+
+FLOPS = 2 * B * I * FS * O * FS + 2 * B * O * LQ * I * LS * D
+
+
+def tile_localcrossattention_pa_t_e_kernel(
+    tc, scores, final_encoder_out, WV_w_words, WV_w_scales, WV_b, out
+):
+    nc = tc.nc
+    score_rows = scores.rearrange("b o (t a) q k -> (b o t) (a q k)", a=A)
+    enc_rows = final_encoder_out.rearrange("b (i l) d -> (b i) (l d)", i=I)
+    out_view = out.rearrange("(J g) (o q) d -> g o q J d", g=B_PASS, o=O)
+
+    with ExitStack() as ctx:
+        const = ctx.enter_context(tc.tile_pool(name="const", bufs=1))
+        two = ctx.enter_context(tc.tile_pool(name="two", bufs=2))
+        three = ctx.enter_context(tc.tile_pool(name="three", bufs=3))
+        four = ctx.enter_context(tc.tile_pool(name="four", bufs=4))
+        ps_turned = ctx.enter_context(tc.psum_pool(name="ps_turned", bufs=4))
+        ps_v = ctx.enter_context(tc.psum_pool(name="ps_v", bufs=2))
+        ps_out = ctx.enter_context(tc.psum_pool(name="ps_out", bufs=2))
+        ctx.enter_context(tc.manual_schedule())
+
+        score_tiles, exp_tiles, recip_tiles, attn_tiles, attn_grouped_tiles = {}, {}, {}, {}, {}
+        attn_operands, enc_tiles, enc_grouped_tiles, enc_operands = {}, {}, {}, {}
+        v_tiles, v_grouped_tiles, v_operands, out_banks, result_tiles = {}, {}, {}, {}, {}
+
+        def load_scores(tile):
+            if tile >= N_TILES:
+                return
+            s_sb = three.tile([P, A * LQ * LS], BF16)
+            nc.sync.dma_start(out=s_sb[:], in_=score_rows[P * tile : P * (tile + 1), :])
+            score_tiles[tile] = s_sb
+
+        def load_enc(group):
+            if group >= N_GROUPS:
+                return
+            enc_sb = two.tile([P, ROW_TILES, FS], BF16)
+            first = ROW_TILES * P * group
+            nc.sync.dma_start(
+                out=enc_sb[:],
+                in_=enc_rows[first : first + ROW_TILES * P, :].rearrange("(r x) f -> x r f", x=P),
+            )
+            enc_tiles[group] = enc_sb
+
+        def turn_enc(group):
+            if not 0 <= group < N_GROUPS:
+                return
+            enc_sb = enc_tiles[group]
+            enc_grouped = two.tile([P, A, ROW_TILES, B_ROWS * PACK, PACK], BF16, align_bytes=64)
+            for half in range(ROW_TILES // 2):
+                enc_t = ps_turned.tile([P, 2, 2, P], F32, tag="turned")
+                for r in range(2):
+                    words = enc_sb[:, 2 * half + r, :].bitcast(F32)
+                    for u in range(2):
+                        nc.tensor.transpose(enc_t[:, r, u, :], words[:, u : FS // 2 : 2], ident_f32[:])
+                for r in range(2):
+                    nc.scalar.copy(
+                        out=enc_grouped[:, :, 2 * half + r, :, :].bitcast(F32),
+                        in_=enc_t[:, r, :, :].rearrange("p u (bt a) -> p a bt u", a=A),
+                    )
+            enc_grouped_tiles[group] = enc_grouped
+
+        def quantise_enc(group):
+            if not 0 <= group < N_GROUPS:
+                return
+            enc_codes = two.tile([P, A * P], U32, align_bytes=64)
+            enc_scales = two.tile([P, A * P], U8, align_bytes=64)
+            nc.vector.quantize_mx(
+                out=enc_codes[:].bitcast(FP8X4),
+                scales=enc_scales[:],
+                in_=enc_grouped_tiles[group][:].rearrange("p a r m t -> p (a r m t)"),
+            )
+            enc_operands[group] = (enc_codes, enc_scales)
+
+        def project(unit):
+            if not 0 <= unit < N_UNITS:
+                return
+            group, o = divmod(unit, O)
+            enc_codes, enc_scales = enc_operands[group]
+            v_sb = two.tile([P, D, A, LS], BF16)
+            for a in range(A):
+                rows = slice(P * a, P * (a + 1))
+                v_ps = ps_v.tile([P, FS], F32)
+                nc.tensor.matmul_mx(
+                    out=v_ps[:],
+                    lhsT=enc_codes[:, rows].bitcast(FP8X4),
+                    lhsT_scale=enc_scales[:, rows],
+                    rhs=w_words[:, o, :].bitcast(FP8X4),
+                    rhs_scale=w_scales[:, o, :],
+                    start=True,
+                    stop=True,
+                )
+                nc.vector.tensor_tensor(
+                    out=v_sb[:, :, a, :],
+                    in0=v_ps[:].rearrange("p (k d) -> p d k", d=D),
+                    in1=bias_dk[:, o, :, :],
+                    op=ALU.add,
+                )
+            v_tiles[unit] = v_sb
+
+        def turn_v(unit):
+            if not 0 <= unit < N_UNITS:
+                return
+            v_sb = v_tiles[unit]
+            v_grouped = two.tile([P, B_GROUP // B_MOVING, D, B_MOVING * PACK], BF16, align_bytes=64)
+            for c in range(D // D_CHUNK):
+                v_t = ps_turned.tile([P, B_GROUP // B_MOVING, D_CHUNK, B_MOVING * PACK], BF16, tag="turned")
+                for d in range(D_CHUNK):
+                    nc.tensor.transpose(
+                        v_t[:, :, d, :],
+                        v_sb[:, D_CHUNK * c + d, :, :].rearrange("p a k -> p (a k)"),
+                        ident_bf16[:],
+                    )
+                nc.scalar.copy(out=v_grouped[:, :, D_CHUNK * c : D_CHUNK * (c + 1), :], in_=v_t[:])
+            v_grouped_tiles[unit] = v_grouped
+
+        def quantise_v(unit):
+            if not 0 <= unit < N_UNITS:
+                return
+            v_codes = four.tile([P, B_GROUP * D], U32, align_bytes=64)
+            v_scales = four.tile([P, B_GROUP * D], U8, align_bytes=64)
+            nc.vector.quantize_mx(
+                out=v_codes[:].bitcast(FP8X4),
+                scales=v_scales[:],
+                in_=v_grouped_tiles[unit][:].rearrange("p e d m -> p (e d m)"),
+            )
+            v_operands[unit] = (v_codes, v_scales)
+
+        def exp_and_sums(tile):
+            if not 0 <= tile < N_TILES:
+                return
+            s_view = score_tiles[tile][:].rearrange("x (a q k) -> x q a k", a=A, q=LQ)
+            e_sb = three.tile([P, LQ, A, LS], F32)
+            denom = two.tile([P, LQ * A], F32)
+            for c in range(N_CHUNKS):
+                queries = slice(Q_CHUNK * c, Q_CHUNK * (c + 1))
+                nc.scalar.activation(out=e_sb[:, queries, :, :], in_=s_view[:, queries, :, :], func=ACT.Exp)
+                nc.vector.tensor_reduce(
+                    out=denom[:, Q_CHUNK * A * c : Q_CHUNK * A * (c + 1)],
+                    in_=e_sb[:, queries, :, :].rearrange("x q a k -> x (q a) k"),
+                    axis=AXIS.X,
+                    op=ALU.add,
+                )
+            nc.vector.tensor_scalar_add(out=denom[:], in0=denom[:], scalar1=EPS)
+            recip = four.tile([P, LQ * A], F32)
+            nc.vector.reciprocal(out=recip[:], in_=denom[:])
+            exp_tiles[tile] = e_sb
+            recip_tiles[tile] = recip
+
+        def divide(tile):
+            if not 0 <= tile < N_TILES:
+                return
+            attn_sb = two.tile([P, LQ, A * LS], BF16)
+            for c in range(N_CHUNKS):
+                queries = slice(Q_CHUNK * c, Q_CHUNK * (c + 1))
+                nc.gpsimd.tensor_tensor(
+                    out=attn_sb[:, queries, :].rearrange("x q (a k) -> x (q a) k", k=LS),
+                    in0=exp_tiles[tile][:, queries, :, :].rearrange("x q a k -> x (q a) k"),
+                    in1=recip_tiles[tile][:, Q_CHUNK * A * c : Q_CHUNK * A * (c + 1)]
+                    .unsqueeze(2)
+                    .to_broadcast([P, Q_CHUNK * A, LS]),
+                    op=ALU.mult,
+                )
+            attn_tiles[tile] = attn_sb
+
+        def turn_attn(tile):
+            if not 0 <= tile < N_TILES:
+                return
+            attn_grouped = two.tile([P, O * B_TILE, LQ, PACK], BF16, align_bytes=64)
+            for c in range(N_CHUNKS):
+                attn_t = ps_turned.tile([P, O, B_TILE, Q_CHUNK, PACK], BF16, tag="turned")
+                for q in range(Q_CHUNK):
+                    nc.tensor.transpose(
+                        attn_t[:, :, :, q, :].rearrange("p o b t -> p b o t"),
+                        attn_tiles[tile][:, Q_CHUNK * c + q, :],
+                        ident_bf16[:],
+                    )
+                nc.scalar.copy(
+                    out=attn_grouped[:, :, Q_CHUNK * c : Q_CHUNK * (c + 1), :],
+                    in_=attn_t[:].rearrange("p o b q t -> p (o b) q t"),
+                )
+            attn_grouped_tiles[tile] = attn_grouped
+
+        def quantise_attn(tile):
+            if not 0 <= tile < N_TILES:
+                return
+            attn_codes = two.tile([P, O * B_TILE * LQ], U32, align_bytes=64)
+            attn_scales = two.tile([P, O * B_TILE * LQ], U8, align_bytes=64)
+            nc.vector.quantize_mx(
+                out=attn_codes[:].bitcast(FP8X4),
+                scales=attn_scales[:],
+                in_=attn_grouped_tiles[tile][:].rearrange("p c q t -> p (c q t)"),
+            )
+            attn_operands[tile] = (attn_codes, attn_scales)
+
+        def weigh(tile):
+            if not 0 <= tile < N_TILES:
+                return
+            attn_codes, attn_scales = attn_operands[tile]
+            for o in range(O):
+                v_codes, v_scales = v_operands[(B_TILE * tile // B_GROUP) * O + o]
+                out_ps = ps_out.tile([P, PASSES, P], F32)
+                for j in range(PASSES):
+                    a_first = (o * B_TILE + B_PASS * j) * LQ
+                    eight = (B_TILE * tile + B_PASS * j) % B_GROUP // B_MOVING
+                    nc.tensor.matmul_mx(
+                        out=out_ps[:, j, :],
+                        lhsT=attn_codes[:, a_first : a_first + P].bitcast(FP8X4),
+                        lhsT_scale=attn_scales[:, a_first : a_first + P],
+                        rhs=v_codes[:, P * eight : P * (eight + 1)].bitcast(FP8X4),
+                        rhs_scale=v_scales[:, P * eight : P * (eight + 1)],
+                        start=True,
+                        stop=True,
+                    )
+                out_banks[(tile, o)] = out_ps
+
+        def keep_and_store(tile):
+            if not 0 <= tile < N_TILES:
+                return
+            batch, place = divmod(tile, STORE_TILES)
+            if place == 0:
+                results = two.tile([P, O, STORE_TILES * PASSES, B_PASS, D], F32)
+                result_tiles[batch] = results
+            results = result_tiles[batch]
+            for o in range(O):
+                halves = out_banks[(tile, o)][:].rearrange(
+                    "p (jh jl) (d bh bl) -> p jl bh jh bl d", jl=2, bh=2, bl=B_PASS
+                )
+                for half in range(2):
+                    nc.scalar.mul(
+                        out=results[:, o, PASSES * place + half : PASSES * (place + 1) : 2, :, :],
+                        in_=halves[:, half, half],
+                        mul=1.0 / math.sqrt(D),
+                    )
+            if place == STORE_TILES - 1:
+                passes = slice(STORE_TILES * PASSES * batch, STORE_TILES * PASSES * (batch + 1))
+                for o in range(O):
+                    for g in range(B_PASS):
+                        nc.scalar.dma_start(
+                            out=out_view[g, o, :, passes, :],
+                            in_=results[LQ * g : LQ * (g + 1), o, :, g, :],
+                        )
+
+        ident_f32 = const.tile([P, P], F32)
+        make_identity(nc, ident_f32[:])
+        ident_bf16 = const.tile([P, P], BF16)
+        make_identity(nc, ident_bf16[:])
+        w_scales = const.tile([P, O, FS], U8, align_bytes=64)
+        nc.vector.memset(w_scales[:].bitcast(I32), 0)
+
+        load_enc(0)
+        load_scores(0)
+        w_words = const.tile([P, O, FS], U32, align_bytes=64)
+        nc.sync.dma_start(
+            out=w_words[:].bitcast(I32),
+            in_=WV_w_words.rearrange("o p n t -> p o (n t)").bitcast(I32),
+        )
+        for quadrant in range(4):
+            nc.sync.dma_start(
+                out=w_scales[32 * quadrant : 32 * quadrant + 4, :, :].bitcast(I32),
+                in_=WV_w_scales[:, 4 * quadrant : 4 * quadrant + 4, :]
+                .rearrange("o r n -> r o n")
+                .bitcast(I32),
+            )
+        bias_rows = const.tile([P, O * FS], BF16)
+        nc.sync.dma_start(out=bias_rows[:], in_=WV_b.rearrange("o n -> (o n)").partition_broadcast(P))
+        bias_dk = const.tile([P, O, D, LS], F32)
+        nc.gpsimd.tensor_copy(
+            out=bias_dk[:], in_=bias_rows[:].rearrange("p (o k d) -> p o d k", o=O, k=LS)
+        )
+        load_scores(1)
+
+        for n in range(-2, N_TILES + 1):
+            load_scores(n + 4)
+            if n % 2 == 0:
+                load_enc(n // 2 + 2)
+            turn_attn(n - 1)
+            turn_v(n)
+            if n % 2 == 0:
+                turn_enc(n // 2 + 1)
+            quantise_attn(n - 1)
+            quantise_v(n)
+            if n % 2 == 0:
+                quantise_enc(n // 2 + 1)
+            weigh(n - 1)
+            project(n + 1)
+            exp_and_sums(n + 2)
+            keep_and_store(n - 1)
+            divide(n)

@@ -28,6 +28,8 @@ N_CHUNKS = LQ // Q_CHUNK
 B_PASS = P // LQ
 PASSES = B_TILE // B_PASS
 STORE_TILES = 4
+CHUNKS_ON_GPSIMD = 3
+HALF = N_CHUNKS // 2
 
 B_GROUP = P // PACK
 N_GROUPS = B // B_GROUP
@@ -53,12 +55,14 @@ def tile_localcrossattention_pa_t_e_kernel(
         two = ctx.enter_context(tc.tile_pool(name="two", bufs=2))
         three = ctx.enter_context(tc.tile_pool(name="three", bufs=3))
         four = ctx.enter_context(tc.tile_pool(name="four", bufs=4))
+        five = ctx.enter_context(tc.tile_pool(name="five", bufs=5))
         ps_turned = ctx.enter_context(tc.psum_pool(name="ps_turned", bufs=4))
         ps_v = ctx.enter_context(tc.psum_pool(name="ps_v", bufs=2))
         ps_out = ctx.enter_context(tc.psum_pool(name="ps_out", bufs=2))
         ctx.enter_context(tc.manual_schedule())
 
-        score_tiles, exp_tiles, recip_tiles, attn_tiles, attn_grouped_tiles = {}, {}, {}, {}, {}
+        score_tiles, exp_tiles, denom_tiles, recip_tiles, attn_tiles = {}, {}, {}, {}, {}
+        attn_grouped_tiles = {}
         attn_operands, enc_tiles, enc_grouped_tiles, enc_operands = {}, {}, {}, {}
         v_tiles, v_grouped_tiles, v_operands, out_banks, result_tiles = {}, {}, {}, {}, {}
 
@@ -155,8 +159,8 @@ def tile_localcrossattention_pa_t_e_kernel(
         def quantise_v(unit):
             if not 0 <= unit < N_UNITS:
                 return
-            v_codes = four.tile([P, B_GROUP * D], U32, align_bytes=64)
-            v_scales = four.tile([P, B_GROUP * D], U8, align_bytes=64)
+            v_codes = five.tile([P, B_GROUP * D], U32, align_bytes=64)
+            v_scales = five.tile([P, B_GROUP * D], U8, align_bytes=64)
             nc.vector.quantize_mx(
                 out=v_codes[:].bitcast(FP8X4),
                 scales=v_scales[:],
@@ -164,13 +168,18 @@ def tile_localcrossattention_pa_t_e_kernel(
             )
             v_operands[unit] = (v_codes, v_scales)
 
-        def exp_and_sums(tile):
+        def exp_and_sums(tile, first_chunk):
             if not 0 <= tile < N_TILES:
                 return
+            if first_chunk == 0:
+                e_sb = three.tile([P, LQ, A, LS], F32)
+                denom = two.tile([P, LQ * A], F32)
+                exp_tiles[tile] = e_sb
+                denom_tiles[tile] = denom
             s_view = score_tiles[tile][:].rearrange("x (a q k) -> x q a k", a=A, q=LQ)
-            e_sb = three.tile([P, LQ, A, LS], F32)
-            denom = two.tile([P, LQ * A], F32)
-            for c in range(N_CHUNKS):
+            e_sb = exp_tiles[tile]
+            denom = denom_tiles[tile]
+            for c in range(first_chunk, first_chunk + HALF):
                 queries = slice(Q_CHUNK * c, Q_CHUNK * (c + 1))
                 nc.scalar.activation(out=e_sb[:, queries, :, :], in_=s_view[:, queries, :, :], func=ACT.Exp)
                 nc.vector.tensor_reduce(
@@ -179,10 +188,11 @@ def tile_localcrossattention_pa_t_e_kernel(
                     axis=AXIS.X,
                     op=ALU.add,
                 )
+            if first_chunk + HALF < N_CHUNKS:
+                return
             nc.vector.tensor_scalar_add(out=denom[:], in0=denom[:], scalar1=EPS)
             recip = four.tile([P, LQ * A], F32)
             nc.vector.reciprocal(out=recip[:], in_=denom[:])
-            exp_tiles[tile] = e_sb
             recip_tiles[tile] = recip
 
         def divide(tile):
@@ -191,7 +201,8 @@ def tile_localcrossattention_pa_t_e_kernel(
             attn_sb = two.tile([P, LQ, A * LS], BF16)
             for c in range(N_CHUNKS):
                 queries = slice(Q_CHUNK * c, Q_CHUNK * (c + 1))
-                nc.gpsimd.tensor_tensor(
+                engine = nc.gpsimd if c < CHUNKS_ON_GPSIMD else nc.vector
+                engine.tensor_tensor(
                     out=attn_sb[:, queries, :].rearrange("x q (a k) -> x (q a) k", k=LS),
                     in0=exp_tiles[tile][:, queries, :, :].rearrange("x q a k -> x (q a) k"),
                     in1=recip_tiles[tile][:, Q_CHUNK * A * c : Q_CHUNK * A * (c + 1)]
@@ -235,14 +246,16 @@ def tile_localcrossattention_pa_t_e_kernel(
             if not 0 <= tile < N_TILES:
                 return
             attn_codes, attn_scales = attn_operands[tile]
+            for parity in range(2):
+                out_ps = ps_out.tile([P, O, PASSES // 2, P], F32)
+                out_banks[(tile, parity)] = out_ps
             for o in range(O):
                 v_codes, v_scales = v_operands[(B_TILE * tile // B_GROUP) * O + o]
-                out_ps = ps_out.tile([P, PASSES, P], F32)
                 for j in range(PASSES):
                     a_first = (o * B_TILE + B_PASS * j) * LQ
                     eight = (B_TILE * tile + B_PASS * j) % B_GROUP // B_MOVING
                     nc.tensor.matmul_mx(
-                        out=out_ps[:, j, :],
+                        out=out_banks[(tile, j % 2)][:, o, j // 2, :],
                         lhsT=attn_codes[:, a_first : a_first + P].bitcast(FP8X4),
                         lhsT_scale=attn_scales[:, a_first : a_first + P],
                         rhs=v_codes[:, P * eight : P * (eight + 1)].bitcast(FP8X4),
@@ -250,7 +263,6 @@ def tile_localcrossattention_pa_t_e_kernel(
                         start=True,
                         stop=True,
                     )
-                out_banks[(tile, o)] = out_ps
 
         def keep_and_store(tile):
             if not 0 <= tile < N_TILES:
@@ -260,16 +272,15 @@ def tile_localcrossattention_pa_t_e_kernel(
                 results = two.tile([P, O, STORE_TILES * PASSES, B_PASS, D], F32)
                 result_tiles[batch] = results
             results = result_tiles[batch]
-            for o in range(O):
-                halves = out_banks[(tile, o)][:].rearrange(
-                    "p (jh jl) (d bh bl) -> p jl bh jh bl d", jl=2, bh=2, bl=B_PASS
+            for parity in range(2):
+                halves = out_banks[(tile, parity)][:].rearrange(
+                    "p o j (d bh bl) -> p bh o j bl d", bh=2, bl=B_PASS
                 )
-                for half in range(2):
-                    nc.scalar.mul(
-                        out=results[:, o, PASSES * place + half : PASSES * (place + 1) : 2, :, :],
-                        in_=halves[:, half, half],
-                        mul=1.0 / math.sqrt(D),
-                    )
+                nc.scalar.mul(
+                    out=results[:, :, PASSES * place + parity : PASSES * (place + 1) : 2, :, :],
+                    in_=halves[:, parity],
+                    mul=1.0 / math.sqrt(D),
+                )
             if place == STORE_TILES - 1:
                 passes = slice(STORE_TILES * PASSES * batch, STORE_TILES * PASSES * (batch + 1))
                 for o in range(O):
@@ -286,8 +297,8 @@ def tile_localcrossattention_pa_t_e_kernel(
         w_scales = const.tile([P, O, FS], U8, align_bytes=64)
         nc.vector.memset(w_scales[:].bitcast(I32), 0)
 
-        load_enc(0)
         load_scores(0)
+        load_enc(0)
         w_words = const.tile([P, O, FS], U32, align_bytes=64)
         nc.sync.dma_start(
             out=w_words[:].bitcast(I32),
@@ -308,10 +319,15 @@ def tile_localcrossattention_pa_t_e_kernel(
         )
         load_scores(1)
 
-        for n in range(-2, N_TILES + 1):
+        for n in range(-2, N_TILES + 2):
             load_scores(n + 4)
             if n % 2 == 0:
                 load_enc(n // 2 + 2)
+            weigh(n - 2)
+            project(n + 1)
+            exp_and_sums(n + 2, 0)
+            keep_and_store(n - 2)
+            divide(n)
             turn_attn(n - 1)
             turn_v(n)
             if n % 2 == 0:
@@ -320,8 +336,4 @@ def tile_localcrossattention_pa_t_e_kernel(
             quantise_v(n)
             if n % 2 == 0:
                 quantise_enc(n // 2 + 1)
-            weigh(n - 1)
-            project(n + 1)
-            exp_and_sums(n + 2)
-            keep_and_store(n - 1)
-            divide(n)
+            exp_and_sums(n + 2, HALF)

@@ -28,8 +28,6 @@ N_CHUNKS = LQ // Q_CHUNK
 B_PASS = P // LQ
 PASSES = B_TILE // B_PASS
 STORE_TILES = 4
-CHUNKS_ON_GPSIMD = 3
-HALF = N_CHUNKS // 2
 
 B_GROUP = P // PACK
 N_GROUPS = B // B_GROUP
@@ -55,14 +53,11 @@ def tile_localcrossattention_pa_t_e_kernel(
         two = ctx.enter_context(tc.tile_pool(name="two", bufs=2))
         three = ctx.enter_context(tc.tile_pool(name="three", bufs=3))
         four = ctx.enter_context(tc.tile_pool(name="four", bufs=4))
-        five = ctx.enter_context(tc.tile_pool(name="five", bufs=5))
         ps_turned = ctx.enter_context(tc.psum_pool(name="ps_turned", bufs=4))
         ps_v = ctx.enter_context(tc.psum_pool(name="ps_v", bufs=2))
         ps_out = ctx.enter_context(tc.psum_pool(name="ps_out", bufs=2))
-        ctx.enter_context(tc.manual_schedule())
 
-        score_tiles, exp_tiles, denom_tiles, recip_tiles, attn_tiles = {}, {}, {}, {}, {}
-        attn_grouped_tiles = {}
+        score_tiles, exp_tiles, recip_tiles, attn_tiles, attn_grouped_tiles = {}, {}, {}, {}, {}
         attn_operands, enc_tiles, enc_grouped_tiles, enc_operands = {}, {}, {}, {}
         v_tiles, v_grouped_tiles, v_operands, out_banks, result_tiles = {}, {}, {}, {}, {}
 
@@ -153,14 +148,14 @@ def tile_localcrossattention_pa_t_e_kernel(
                         v_sb[:, D_CHUNK * c + d, :, :].rearrange("p a k -> p (a k)"),
                         ident_bf16[:],
                     )
-                nc.scalar.copy(out=v_grouped[:, :, D_CHUNK * c : D_CHUNK * (c + 1), :], in_=v_t[:])
+                nc.vector.tensor_copy(out=v_grouped[:, :, D_CHUNK * c : D_CHUNK * (c + 1), :], in_=v_t[:])
             v_grouped_tiles[unit] = v_grouped
 
         def quantise_v(unit):
             if not 0 <= unit < N_UNITS:
                 return
-            v_codes = five.tile([P, B_GROUP * D], U32, align_bytes=64)
-            v_scales = five.tile([P, B_GROUP * D], U8, align_bytes=64)
+            v_codes = four.tile([P, B_GROUP * D], U32, align_bytes=64)
+            v_scales = four.tile([P, B_GROUP * D], U8, align_bytes=64)
             nc.vector.quantize_mx(
                 out=v_codes[:].bitcast(FP8X4),
                 scales=v_scales[:],
@@ -168,18 +163,13 @@ def tile_localcrossattention_pa_t_e_kernel(
             )
             v_operands[unit] = (v_codes, v_scales)
 
-        def exp_and_sums(tile, first_chunk):
+        def exp_and_sums(tile):
             if not 0 <= tile < N_TILES:
                 return
-            if first_chunk == 0:
-                e_sb = three.tile([P, LQ, A, LS], F32)
-                denom = two.tile([P, LQ * A], F32)
-                exp_tiles[tile] = e_sb
-                denom_tiles[tile] = denom
             s_view = score_tiles[tile][:].rearrange("x (a q k) -> x q a k", a=A, q=LQ)
-            e_sb = exp_tiles[tile]
-            denom = denom_tiles[tile]
-            for c in range(first_chunk, first_chunk + HALF):
+            e_sb = three.tile([P, LQ, A, LS], F32)
+            denom = two.tile([P, LQ * A], F32)
+            for c in range(N_CHUNKS):
                 queries = slice(Q_CHUNK * c, Q_CHUNK * (c + 1))
                 nc.scalar.activation(out=e_sb[:, queries, :, :], in_=s_view[:, queries, :, :], func=ACT.Exp)
                 nc.vector.tensor_reduce(
@@ -188,11 +178,10 @@ def tile_localcrossattention_pa_t_e_kernel(
                     axis=AXIS.X,
                     op=ALU.add,
                 )
-            if first_chunk + HALF < N_CHUNKS:
-                return
             nc.vector.tensor_scalar_add(out=denom[:], in0=denom[:], scalar1=EPS)
             recip = four.tile([P, LQ * A], F32)
             nc.vector.reciprocal(out=recip[:], in_=denom[:])
+            exp_tiles[tile] = e_sb
             recip_tiles[tile] = recip
 
         def divide(tile):
@@ -201,8 +190,7 @@ def tile_localcrossattention_pa_t_e_kernel(
             attn_sb = two.tile([P, LQ, A * LS], BF16)
             for c in range(N_CHUNKS):
                 queries = slice(Q_CHUNK * c, Q_CHUNK * (c + 1))
-                engine = nc.gpsimd if c < CHUNKS_ON_GPSIMD else nc.vector
-                engine.tensor_tensor(
+                nc.gpsimd.tensor_tensor(
                     out=attn_sb[:, queries, :].rearrange("x q (a k) -> x (q a) k", k=LS),
                     in0=exp_tiles[tile][:, queries, :, :].rearrange("x q a k -> x (q a) k"),
                     in1=recip_tiles[tile][:, Q_CHUNK * A * c : Q_CHUNK * A * (c + 1)]
@@ -297,8 +285,8 @@ def tile_localcrossattention_pa_t_e_kernel(
         w_scales = const.tile([P, O, FS], U8, align_bytes=64)
         nc.vector.memset(w_scales[:].bitcast(I32), 0)
 
-        load_scores(0)
         load_enc(0)
+        load_scores(0)
         w_words = const.tile([P, O, FS], U32, align_bytes=64)
         nc.sync.dma_start(
             out=w_words[:].bitcast(I32),
@@ -319,15 +307,10 @@ def tile_localcrossattention_pa_t_e_kernel(
         )
         load_scores(1)
 
-        for n in range(-2, N_TILES + 2):
+        for n in range(-2, N_TILES + 1):
             load_scores(n + 4)
             if n % 2 == 0:
                 load_enc(n // 2 + 2)
-            weigh(n - 2)
-            project(n + 1)
-            exp_and_sums(n + 2, 0)
-            keep_and_store(n - 2)
-            divide(n)
             turn_attn(n - 1)
             turn_v(n)
             if n % 2 == 0:
@@ -336,4 +319,8 @@ def tile_localcrossattention_pa_t_e_kernel(
             quantise_v(n)
             if n % 2 == 0:
                 quantise_enc(n // 2 + 1)
-            exp_and_sums(n + 2, HALF)
+            weigh(n - 1)
+            project(n + 1)
+            exp_and_sums(n + 2)
+            keep_and_store(n - 1)
+            divide(n)

import math
from contextlib import ExitStack

import concourse.mybir as mybir
from concourse.masks import make_identity

F32 = mybir.dt.float32
BF16 = mybir.dt.bfloat16
I32 = mybir.dt.int32
U32 = mybir.dt.uint32
U8 = mybir.dt.uint8
FP8X4 = mybir.dt.float8_e4m3fn_x4
ACT = mybir.ActivationFunctionType
ALU = mybir.AluOpType
AXIS = mybir.AxisListType

P = 128
PACK = 4
B, O, I, LQ, LS, D = 256, 2, 16, 32, 32, 16
FS = LS * D
EPS = 1e-5
A = I // PACK

B_TILE = P // (O * PACK)
N_TILES = B // B_TILE
Q_CHUNK = 8
N_CHUNKS = LQ // Q_CHUNK
B_PASS = P // LQ
PASSES = B_TILE // B_PASS
STORE_TILES = 4

B_GROUP = P // PACK
N_GROUPS = B // B_GROUP
ROW_TILES = B_GROUP * I // P
B_ROWS = P // I
N_UNITS = N_GROUPS * O
B_MOVING = P // D
D_CHUNK = 8

FLOPS = 2 * B * I * FS * O * FS + 2 * B * O * LQ * I * LS * D


def tile_localcrossattention_pa_t_e_kernel(
    tc, scores, final_encoder_out, WV_w_words, WV_w_scales, WV_b, out
):
    nc = tc.nc
    score_rows = scores.rearrange("b o (t a) q k -> (b o t) (a q k)", a=A)
    enc_rows = final_encoder_out.rearrange("b (i l) d -> (b i) (l d)", i=I)
    out_view = out.rearrange("(J g) (o q) d -> g o q J d", g=B_PASS, o=O)

    with ExitStack() as ctx:
        const = ctx.enter_context(tc.tile_pool(name="const", bufs=1))
        two = ctx.enter_context(tc.tile_pool(name="two", bufs=2))
        three = ctx.enter_context(tc.tile_pool(name="three", bufs=3))
        four = ctx.enter_context(tc.tile_pool(name="four", bufs=4))
        ps_turned = ctx.enter_context(tc.psum_pool(name="ps_turned", bufs=4))
        ps_v = ctx.enter_context(tc.psum_pool(name="ps_v", bufs=2))
        ps_out = ctx.enter_context(tc.psum_pool(name="ps_out", bufs=2))

        score_tiles, exp_tiles, recip_tiles, attn_tiles, attn_grouped_tiles = {}, {}, {}, {}, {}
        attn_operands, enc_tiles, enc_grouped_tiles, enc_operands = {}, {}, {}, {}
        v_tiles, v_grouped_tiles, v_operands, out_banks, result_tiles = {}, {}, {}, {}, {}

        def load_scores(tile):
            if tile >= N_TILES:
                return
            s_sb = three.tile([P, A * LQ * LS], BF16)
            nc.sync.dma_start(out=s_sb[:], in_=score_rows[P * tile : P * (tile + 1), :])
            score_tiles[tile] = s_sb

        def load_enc(group):
            if group >= N_GROUPS:
                return
            enc_sb = two.tile([P, ROW_TILES, FS], BF16)
            first = ROW_TILES * P * group
            nc.sync.dma_start(
                out=enc_sb[:],
                in_=enc_rows[first : first + ROW_TILES * P, :].rearrange("(r x) f -> x r f", x=P),
            )
            enc_tiles[group] = enc_sb

        def turn_enc(group):
            if not 0 <= group < N_GROUPS:
                return
            enc_sb = enc_tiles[group]
            enc_grouped = two.tile([P, A, ROW_TILES, B_ROWS * PACK, PACK], BF16, align_bytes=64)
            for half in range(ROW_TILES // 2):
                enc_t = ps_turned.tile([P, 2, 2, P], F32, tag="turned")
                for r in range(2):
                    words = enc_sb[:, 2 * half + r, :].bitcast(F32)
                    for u in range(2):
                        nc.tensor.transpose(enc_t[:, r, u, :], words[:, u : FS // 2 : 2], ident_f32[:])
                for r in range(2):
                    nc.scalar.copy(
                        out=enc_grouped[:, :, 2 * half + r, :, :].bitcast(F32),
                        in_=enc_t[:, r, :, :].rearrange("p u (bt a) -> p a bt u", a=A),
                    )
            enc_grouped_tiles[group] = enc_grouped

        def quantise_enc(group):
            if not 0 <= group < N_GROUPS:
                return
            enc_codes = two.tile([P, A * P], U32, align_bytes=64)
            enc_scales = two.tile([P, A * P], U8, align_bytes=64)
            nc.vector.quantize_mx(
                out=enc_codes[:].bitcast(FP8X4),
                scales=enc_scales[:],
                in_=enc_grouped_tiles[group][:].rearrange("p a r m t -> p (a r m t)"),
            )
            enc_operands[group] = (enc_codes, enc_scales)

        def project(unit):
            if not 0 <= unit < N_UNITS:
                return
            group, o = divmod(unit, O)
            enc_codes, enc_scales = enc_operands[group]
            v_sb = two.tile([P, D, A, LS], BF16)
            for a in range(A):
                rows = slice(P * a, P * (a + 1))
                v_ps = ps_v.tile([P, FS], F32)
                nc.tensor.matmul_mx(
                    out=v_ps[:],
                    lhsT=enc_codes[:, rows].bitcast(FP8X4),
                    lhsT_scale=enc_scales[:, rows],
                    rhs=w_words[:, o, :].bitcast(FP8X4),
                    rhs_scale=w_scales[:, o, :],
                    start=True,
                    stop=True,
                )
                nc.vector.tensor_tensor(
                    out=v_sb[:, :, a, :],
                    in0=v_ps[:].rearrange("p (k d) -> p d k", d=D),
                    in1=bias_dk[:, o, :, :],
                    op=ALU.add,
                )
            v_tiles[unit] = v_sb

        def turn_v(unit):
            if not 0 <= unit < N_UNITS:
                return
            v_sb = v_tiles[unit]
            v_grouped = two.tile([P, B_GROUP // B_MOVING, D, B_MOVING * PACK], BF16, align_bytes=64)
            for c in range(D // D_CHUNK):
                v_t = ps_turned.tile([P, B_GROUP // B_MOVING, D_CHUNK, B_MOVING * PACK], BF16, tag="turned")
                for d in range(D_CHUNK):
                    nc.tensor.transpose(
                        v_t[:, :, d, :],
                        v_sb[:, D_CHUNK * c + d, :, :].rearrange("p a k -> p (a k)"),
                        ident_bf16[:],
                    )
                nc.vector.tensor_copy(out=v_grouped[:, :, D_CHUNK * c : D_CHUNK * (c + 1), :], in_=v_t[:])
            v_grouped_tiles[unit] = v_grouped

        def quantise_v(unit):
            if not 0 <= unit < N_UNITS:
                return
            v_codes = four.tile([P, B_GROUP * D], U32, align_bytes=64)
            v_scales = four.tile([P, B_GROUP * D], U8, align_bytes=64)
            nc.vector.quantize_mx(
                out=v_codes[:].bitcast(FP8X4),
                scales=v_scales[:],
                in_=v_grouped_tiles[unit][:].rearrange("p e d m -> p (e d m)"),
            )
            v_operands[unit] = (v_codes, v_scales)

        def exp_and_sums(tile):
            if not 0 <= tile < N_TILES:
                return
            s_view = score_tiles[tile][:].rearrange("x (a q k) -> x q a k", a=A, q=LQ)
            e_sb = three.tile([P, LQ, A, LS], F32)
            denom = two.tile([P, LQ * A], F32)
            for c in range(N_CHUNKS):
                queries = slice(Q_CHUNK * c, Q_CHUNK * (c + 1))
                nc.scalar.activation(out=e_sb[:, queries, :, :], in_=s_view[:, queries, :, :], func=ACT.Exp)
                nc.vector.tensor_reduce(
                    out=denom[:, Q_CHUNK * A * c : Q_CHUNK * A * (c + 1)],
                    in_=e_sb[:, queries, :, :].rearrange("x q a k -> x (q a) k"),
                    axis=AXIS.X,
                    op=ALU.add,
                )
            nc.vector.tensor_scalar_add(out=denom[:], in0=denom[:], scalar1=EPS)
            recip = four.tile([P, LQ * A], F32)
            nc.vector.reciprocal(out=recip[:], in_=denom[:])
            exp_tiles[tile] = e_sb
            recip_tiles[tile] = recip

        def divide(tile):
            if not 0 <= tile < N_TILES:
                return
            attn_sb = two.tile([P, LQ, A * LS], BF16)
            for c in range(N_CHUNKS):
                queries = slice(Q_CHUNK * c, Q_CHUNK * (c + 1))
                nc.gpsimd.tensor_tensor(
                    out=attn_sb[:, queries, :].rearrange("x q (a k) -> x (q a) k", k=LS),
                    in0=exp_tiles[tile][:, queries, :, :].rearrange("x q a k -> x (q a) k"),
                    in1=recip_tiles[tile][:, Q_CHUNK * A * c : Q_CHUNK * A * (c + 1)]
                    .unsqueeze(2)
                    .to_broadcast([P, Q_CHUNK * A, LS]),
                    op=ALU.mult,
                )
            attn_tiles[tile] = attn_sb

        def turn_attn(tile):
            if not 0 <= tile < N_TILES:
                return
            attn_grouped = two.tile([P, O * B_TILE, LQ, PACK], BF16, align_bytes=64)
            for c in range(N_CHUNKS):
                attn_t = ps_turned.tile([P, O, B_TILE, Q_CHUNK, PACK], BF16, tag="turned")
                for q in range(Q_CHUNK):
                    nc.tensor.transpose(
                        attn_t[:, :, :, q, :].rearrange("p o b t -> p b o t"),
                        attn_tiles[tile][:, Q_CHUNK * c + q, :],
                        ident_bf16[:],
                    )
                nc.scalar.copy(
                    out=attn_grouped[:, :, Q_CHUNK * c : Q_CHUNK * (c + 1), :],
                    in_=attn_t[:].rearrange("p o b q t -> p (o b) q t"),
                )
            attn_grouped_tiles[tile] = attn_grouped

        def quantise_attn(tile):
            if not 0 <= tile < N_TILES:
                return
            attn_codes = two.tile([P, O * B_TILE * LQ], U32, align_bytes=64)
            attn_scales = two.tile([P, O * B_TILE * LQ], U8, align_bytes=64)
            nc.vector.quantize_mx(
                out=attn_codes[:].bitcast(FP8X4),
                scales=attn_scales[:],
                in_=attn_grouped_tiles[tile][:].rearrange("p c q t -> p (c q t)"),
            )
            attn_operands[tile] = (attn_codes, attn_scales)

        def weigh(tile):
            if not 0 <= tile < N_TILES:
                return
            attn_codes, attn_scales = attn_operands[tile]
            for parity in range(2):
                out_ps = ps_out.tile([P, O, PASSES // 2, P], F32)
                out_banks[(tile, parity)] = out_ps
            for o in range(O):
                v_codes, v_scales = v_operands[(B_TILE * tile // B_GROUP) * O + o]
                for j in range(PASSES):
                    a_first = (o * B_TILE + B_PASS * j) * LQ
                    eight = (B_TILE * tile + B_PASS * j) % B_GROUP // B_MOVING
                    nc.tensor.matmul_mx(
                        out=out_banks[(tile, j % 2)][:, o, j // 2, :],
                        lhsT=attn_codes[:, a_first : a_first + P].bitcast(FP8X4),
                        lhsT_scale=attn_scales[:, a_first : a_first + P],
                        rhs=v_codes[:, P * eight : P * (eight + 1)].bitcast(FP8X4),
                        rhs_scale=v_scales[:, P * eight : P * (eight + 1)],
                        start=True,
                        stop=True,
                    )

        def keep_and_store(tile):
            if not 0 <= tile < N_TILES:
                return
            batch, place = divmod(tile, STORE_TILES)
            if place == 0:
                results = two.tile([P, O, STORE_TILES * PASSES, B_PASS, D], F32)
                result_tiles[batch] = results
            results = result_tiles[batch]
            for parity in range(2):
                halves = out_banks[(tile, parity)][:].rearrange(
                    "p o j (d bh bl) -> p bh o j bl d", bh=2, bl=B_PASS
                )
                nc.scalar.mul(
                    out=results[:, :, PASSES * place + parity : PASSES * (place + 1) : 2, :, :],
                    in_=halves[:, parity],
                    mul=1.0 / math.sqrt(D),
                )
            if place == STORE_TILES - 1:
                passes = slice(STORE_TILES * PASSES * batch, STORE_TILES * PASSES * (batch + 1))
                for o in range(O):
                    for g in range(B_PASS):
                        nc.scalar.dma_start(
                            out=out_view[g, o, :, passes, :],
                            in_=results[LQ * g : LQ * (g + 1), o, :, g, :],
                        )

        ident_f32 = const.tile([P, P], F32)
        make_identity(nc, ident_f32[:])
        ident_bf16 = const.tile([P, P], BF16)
        make_identity(nc, ident_bf16[:])
        w_scales = const.tile([P, O, FS], U8, align_bytes=64)
        nc.vector.memset(w_scales[:].bitcast(I32), 0)

        load_enc(0)
        load_scores(0)
        w_words = const.tile([P, O, FS], U32, align_bytes=64)
        nc.sync.dma_start(
            out=w_words[:].bitcast(I32),
            in_=WV_w_words.rearrange("o p n t -> p o (n t)").bitcast(I32),
        )
        for quadrant in range(4):
            nc.sync.dma_start(
                out=w_scales[32 * quadrant : 32 * quadrant + 4, :, :].bitcast(I32),
                in_=WV_w_scales[:, 4 * quadrant : 4 * quadrant + 4, :]
                .rearrange("o r n -> r o n")
                .bitcast(I32),
            )
        bias_rows = const.tile([P, O * FS], BF16)
        nc.sync.dma_start(out=bias_rows[:], in_=WV_b.rearrange("o n -> (o n)").partition_broadcast(P))
        bias_dk = const.tile([P, O, D, LS], F32)
        nc.gpsimd.tensor_copy(
            out=bias_dk[:], in_=bias_rows[:].rearrange("p (o k d) -> p o d k", o=O, k=LS)
        )
        load_scores(1)

        for n in range(-2, N_TILES + 1):
            load_scores(n + 4)
            if n % 2 == 0:
                load_enc(n // 2 + 2)
            turn_attn(n - 1)
            turn_v(n)
            if n % 2 == 0:
                turn_enc(n // 2 + 1)
            quantise_attn(n - 1)
            quantise_v(n)
            if n % 2 == 0:
                quantise_enc(n // 2 + 1)
            weigh(n - 1)
            project(n + 1)
            exp_and_sums(n + 2)
            keep_and_store(n - 1)
            divide(n)
